import numpy as np
import ml_dtypes


def mxq(x, axis, fmt="e4m3"):
    dtype, down = {"e4m3": (ml_dtypes.float8_e4m3fn, 7), "e5m2": (ml_dtypes.float8_e5m2, 14)}[fmt]
    v = np.moveaxis(np.asarray(x, np.float32).astype(ml_dtypes.bfloat16).astype(np.float64), axis, -1)
    blocks = v.reshape(v.shape[:-1] + (-1, 32))
    amax = np.abs(blocks).max(-1, keepdims=True)
    byte = np.maximum(np.where(amax > 0, np.frexp(amax)[1] - 1 + 127, 0) - down, 1)
    scale = np.exp2(byte - 127.0)
    codes = (blocks / scale).astype(np.float32).astype(dtype).astype(np.float64)
    return np.moveaxis((codes * scale).reshape(v.shape), -1, axis)


WIDE = False


def mx_kscale(k):
    if not WIDE:
        return np.ones(k)
    levels = np.array([10, -10, 5, -5, 0])
    if k % 512:
        return np.exp2(np.random.permutation(np.resize(levels, k // 32))).repeat(32)
    a = np.empty((k // 512, 16))
    for p in range(k // 512):
        a[p, :8] = np.random.permutation(np.resize(levels, 8))
        for g in range(8):
            far = levels[np.abs(levels - a[p, g]) >= 10]
            a[p, g + 8] = far[np.random.randint(len(far))]
    return np.exp2(a.ravel()).repeat(32)


BF16 = ml_dtypes.bfloat16


def bf(x):
    return np.asarray(x, np.float32).astype(BF16)


def f64(x):
    return np.asarray(x).astype(np.float64)


BATCH, SIZE_IN, SIZE_OUT, STEPS = 1024, 2048, 2048, 8


def _build_mask(size_in, size_out, steps):
    inp_el_counts = size_in // steps
    rows = np.arange(size_out)
    count = rows % inp_el_counts
    cols = np.arange(steps)[None, :] * inp_el_counts + count[:, None]
    mask = np.zeros((size_out, size_in), dtype=np.float32)
    mask[rows[:, None], cols] = 1.0
    return mask


def setup_inputs():
    s = mx_kscale(SIZE_IN)
    bound = np.sqrt(3.0 / STEPS)
    return {"x": bf(np.random.standard_normal((BATCH, SIZE_IN)) * s),
            "weights": bf(np.random.uniform(-bound, bound, (SIZE_OUT, SIZE_IN)) / s[None, :]),
            "bias": bf(np.random.uniform(-0.5, 0.5, SIZE_OUT)),
            "mask": bf(_build_mask(SIZE_IN, SIZE_OUT, STEPS))}


def reference(x, weights, bias, mask):
    w = f64(weights) * f64(mask)
    return (mxq(f64(x), 1, "e4m3") @ mxq(w, 1, "e4m3").T) + f64(bias)

@@ -1,0 +1,326 @@
+from contextlib import ExitStack
+
+import concourse.mybir as mybir
+from concourse.masks import make_identity
+
+F32 = mybir.dt.float32
+BF16 = mybir.dt.bfloat16
+U32 = mybir.dt.uint32
+U8 = mybir.dt.uint8
+FP8X4 = mybir.dt.float8_e4m3fn_x4
+ADD = mybir.AluOpType.add
+MULT = mybir.AluOpType.mult
+
+P = 128
+BATCH = 1024
+K = 2048
+FEAT = 2048
+FLOPS = 2 * BATCH * K * FEAT
+
+PASSES = K // 512
+ROWS = 256
+WORDS = K // 2
+N_PIECES = BATCH // ROWS
+N_CHUNKS = FEAT // ROWS
+RAW_BUFS = 8
+HALF_BUFS = 8
+HALF_CHUNKS = 3
+NARROW = [1, 2]
+FINE_TO = 3
+AHEAD_FROM = 1
+LAG = 1
+X_VECTOR_BANKS = []
+STORE_GROUPS = [[0, 1, 2, 3], [4, 5], [6], [7]]
+BIAS_AFTER = 0
+WARM_START = 6
+WARM = {1: 1, 2: 1}
+WHOLE = 2
+SPLIT_CELLS = [(7, 3)]
+
+
+def tile_sparselayer_kernel(tc, x, weights, bias, mask, out):
+    nc = tc.nc
+    x_rows = x.rearrange("(p t) k -> p (t k)", t=BATCH // P)
+    out_rows = out.rearrange("(p t) n -> p t n", t=BATCH // P)
+
+    def w_units(c):
+        if c < HALF_CHUNKS:
+            return [("w", c, 0), ("w", c, 1)]
+        return [("w", c, WHOLE)]
+
+    units = w_units(0) + [("x", tp, WHOLE) for tp in range(N_PIECES)]
+    for c in range(1, N_CHUNKS):
+        units.extend(w_units(c))
+    group_of = {}
+    for gi, chunks in enumerate(STORE_GROUPS):
+        for c in chunks:
+            group_of[c] = gi
+
+    with ExitStack() as ctx:
+        const = ctx.enter_context(tc.tile_pool(name="const", bufs=1))
+        raw_pool = ctx.enter_context(tc.tile_pool(name="raw", bufs=RAW_BUFS))
+        half_pool = ctx.enter_context(tc.tile_pool(name="half", bufs=HALF_BUFS))
+        grouped_pool = ctx.enter_context(tc.tile_pool(name="grouped", bufs=2))
+        wq_pool = ctx.enter_context(tc.tile_pool(name="wq", bufs=3))
+        stage_pool = ctx.enter_context(tc.tile_pool(name="stage", bufs=1))
+        tp_psum = ctx.enter_context(tc.psum_pool(name="tp", bufs=4))
+        mx_psum = ctx.enter_context(tc.psum_pool(name="mx", bufs=4))
+
+        ident = const.tile([P, P], F32)
+        make_identity(nc, ident[:])
+
+        ctx.enter_context(tc.manual_schedule())
+
+        raw = {}
+        state = {"next_load": 0, "raw": RAW_BUFS, "half": HALF_BUFS}
+        bias_row = const.tile([P, FEAT], BF16)
+        nc.vector.memset(bias_row[:], 0.0)
+
+        def load_more():
+            while state["next_load"] < len(units):
+                i = state["next_load"]
+                kind, n, h = units[i]
+                pool_name = "raw" if h == WHOLE else "half"
+                need = 1 if kind == "x" else 2
+                if state[pool_name] < need:
+                    return
+                state[pool_name] -= need
+                state["next_load"] += 1
+                if i == 1:
+                    nc.sync.dma_start(out=bias_row[0:1, :], in_=bias.rearrange("(o n) -> o n", o=1))
+                if kind == "x":
+                    x_raw = raw_pool.tile([P, 2 * K], BF16, tag="raw")
+                    nc.sync.dma_start(out=x_raw[:], in_=x_rows[:, n * 2 * K : (n + 1) * 2 * K])
+                    raw[i] = (x_raw, None)
+                elif h == WHOLE:
+                    rows = slice(n * ROWS, (n + 1) * ROWS)
+                    w_raw = raw_pool.tile([P, 2 * K], BF16, tag="raw")
+                    nc.sync.dma_start(out=w_raw[:], in_=weights[rows, :].rearrange("(p s) k -> p (s k)", s=2))
+                    m_raw = raw_pool.tile([P, 2 * K], BF16, tag="raw")
+                    nc.sync.dma_start(out=m_raw[:], in_=mask[rows, :].rearrange("(p s) k -> p (s k)", s=2))
+                    raw[i] = (w_raw, m_raw)
+                else:
+                    rows = slice(n * ROWS + h * P, n * ROWS + (h + 1) * P)
+                    w_raw = half_pool.tile([P, K], BF16, tag="half")
+                    nc.sync.dma_start(out=w_raw[:], in_=weights[rows, :])
+                    m_raw = half_pool.tile([P, K], BF16, tag="half")
+                    nc.sync.dma_start(out=m_raw[:], in_=mask[rows, :])
+                    raw[i] = (w_raw, m_raw)
+
+        load_more()
+        ones = const.tile([P, P], BF16)
+        nc.vector.memset(ones[:], 1.0)
+        zeros = const.tile([P, 512], BF16)
+        nc.vector.memset(zeros[:], 0.0)
+        bias_all = const.tile([P, FEAT], BF16)
+        junk = mx_psum.tile([P, 512], F32, tag="mx")
+
+        def warm(count):
+            for r in range(count):
+                nc.tensor.matmul(out=junk[:], lhsT=ones[:], rhs=zeros[:], start=True, stop=True)
+
+        def spread_bias():
+            for b in range(FEAT // 1024):
+                spread = mx_psum.tile([P, 1024], BF16, tag="mx")
+                for hb in range(2):
+                    cols = slice(b * 1024 + hb * 512, b * 1024 + (hb + 1) * 512)
+                    nc.tensor.matmul(out=spread[:, hb * 512 : (hb + 1) * 512], lhsT=ones[:], rhs=bias_row[:, cols], start=True, stop=True)
+                nc.scalar.copy(out=bias_all[:, b * 1024 : (b + 1) * 1024], in_=spread[:])
+
+        warm(WARM_START)
+
+        x_codes = const.tile([P, N_PIECES, PASSES * ROWS], U32, align_bytes=64)
+        x_scales = const.tile([P, N_PIECES, PASSES * ROWS], U8, align_bytes=64)
+        w_quantised = {}
+        grouped_of = {}
+        staged = {}
+        banks_open = {}
+        mask_parts = {}
+
+        def n_banks(i):
+            return 4 if units[i][2] == WHOLE else 2
+
+        def is_fine(i):
+            kind, n, h = units[i]
+            return kind == "x" or n <= FINE_TO
+
+        def pool_of(i):
+            return "raw" if units[i][2] == WHOLE else "half"
+
+        for i in range(len(units)):
+            if units[i][0] == "w":
+                mask_parts[i] = n_banks(i) if is_fine(i) else 1
+
+        def apply_mask(i, count):
+            if i >= len(units) or units[i][0] == "x":
+                return
+            kind, n, h = units[i]
+            w_raw, m_raw = raw[i]
+            for r in range(count):
+                if mask_parts[i] == 0:
+                    return
+                b = n_banks(i) - mask_parts[i]
+                mask_parts[i] -= 1
+                if not is_fine(i):
+                    nc.vector.tensor_tensor(out=w_raw[:], in0=w_raw[:], in1=m_raw[:], op=MULT)
+                elif h == WHOLE:
+                    ks = slice(b * 512, (b + 1) * 512)
+                    w3 = w_raw[:].rearrange("p (s k) -> p s k", s=2)
+                    m3 = m_raw[:].rearrange("p (s k) -> p s k", s=2)
+                    nc.vector.tensor_tensor(out=w3[:, :, ks], in0=w3[:, :, ks], in1=m3[:, :, ks], op=MULT)
+                else:
+                    ks = slice(b * 1024, (b + 1) * 1024)
+                    nc.vector.tensor_tensor(out=w_raw[:, ks], in0=w_raw[:, ks], in1=m_raw[:, ks], op=MULT)
+                if mask_parts[i] == 0:
+                    state[pool_of(i)] += 1
+
+        def fill_bank(i, b):
+            kind, n, h = units[i]
+            words = raw[i][0][:].bitcast(F32)
+            bank = tp_psum.tile([P, 4, P], F32, tag="tp")
+            for q in range(4):
+                if h == WHOLE:
+                    first = (q // 2) * WORDS + b * 2 * P + q % 2
+                else:
+                    first = (2 * b + q // 2) * 2 * P + q % 2
+                nc.tensor.transpose(out=bank[:, q, :], in_=words[:, first : first + 2 * P - 1 : 2], identity=ident[:])
+            dst = grouped_of[i][:].bitcast(F32)[:, b * 512 : (b + 1) * 512]
+            if kind == "w" and h == WHOLE:
+                nc.scalar.copy(out=dst.rearrange("p (j q) -> p j q", q=4), in_=bank[:].rearrange("p q j -> p j q"))
+            else:
+                dst = dst.rearrange("p (s j u) -> p s j u", s=2, u=2)
+                src = bank[:].rearrange("p (s u) j -> p s j u", s=2)
+                if kind == "x" and b in X_VECTOR_BANKS:
+                    nc.vector.tensor_copy(out=dst, in_=src)
+                else:
+                    nc.scalar.copy(out=dst, in_=src)
+
+        def quantise(i, b):
+            kind, n, h = units[i]
+            if kind == "x":
+                codes, scales = x_codes[:, n, :], x_scales[:, n, :]
+            else:
+                codes, scales = w_quantised[n][0][:], w_quantised[n][1][:]
+            grouped = grouped_of[i]
+            if b is None:
+                nc.vector.quantize_mx(out=codes.bitcast(FP8X4), scales=scales, in_=grouped[:])
+            elif h == WHOLE:
+                cs = slice(b * 256, (b + 1) * 256)
+                nc.vector.quantize_mx(out=codes[:, cs].bitcast(FP8X4), scales=scales[:, cs], in_=grouped[:, b * 1024 : (b + 1) * 1024])
+            else:
+                for g in (2 * b, 2 * b + 1):
+                    cs = slice(g * ROWS + h * P, g * ROWS + (h + 1) * P)
+                    nc.vector.quantize_mx(out=codes[:, cs].bitcast(FP8X4), scales=scales[:, cs], in_=grouped[:, g * 512 : (g + 1) * 512])
+
+        def prepare(i):
+            kind, n, h = units[i]
+            nb = n_banks(i)
+            grouped = grouped_pool.tile([P, nb * 1024], BF16, tag="grouped", align_bytes=64)
+            grouped_of[i] = grouped
+            if kind == "w" and n not in w_quantised:
+                w_codes = wq_pool.tile([P, PASSES * ROWS], U32, tag="w_codes", align_bytes=64)
+                w_scales = wq_pool.tile([P, PASSES * ROWS], U8, tag="w_scales", align_bytes=64)
+                w_quantised[n] = (w_codes, w_scales)
+            ahead = i + 1 < len(units) and units[i + 1][0] == "w" and units[i + 1][1] >= AHEAD_FROM
+            if ahead:
+                apply_mask(i + 1, 4)
+            if is_fine(i):
+                for b in range(nb):
+                    apply_mask(i, 1)
+                    fill_bank(i, b)
+                    warm(WARM.get(i, 0))
+                    if b >= LAG:
+                        quantise(i, b - LAG)
+                for b in range(nb - LAG, nb):
+                    quantise(i, b)
+            else:
+                apply_mask(i, 1)
+                for b in range(nb):
+                    fill_bank(i, b)
+                quantise(i, None)
+            state[pool_of(i)] += 1
+
+        def multiply_split(c, tp):
+            codes, scales = w_quantised[c]
+            for tt in range(2):
+                small = mx_psum.tile([P, ROWS], F32, tag="mx")
+                for g in range(PASSES):
+                    xs = slice((2 * g + tt) * P, (2 * g + tt + 1) * P)
+                    ws = slice(g * ROWS, (g + 1) * ROWS)
+                    nc.tensor.matmul_mx(
+                        out=small[:],
+                        lhsT=x_codes[:, tp, xs].bitcast(FP8X4),
+                        lhsT_scale=x_scales[:, tp, xs],
+                        rhs=codes[:, ws].bitcast(FP8X4),
+                        rhs_scale=scales[:, ws],
+                        start=(g == 0),
+                        stop=(g == PASSES - 1),
+                    )
+                last = stage_pool.tile([P, ROWS], F32, name="last_%d_%d_%d" % (c, tp, tt))
+                nc.vector.tensor_tensor(out=last[:], in0=small[:], in1=bias_all[:, c * ROWS : (c + 1) * ROWS], op=ADD)
+                nc.sync.dma_start(out=out_rows[:, 2 * tp + tt, c * ROWS : (c + 1) * ROWS], in_=last[:])
+
+        def multiply(c, h, tp):
+            if (c, tp) in SPLIT_CELLS:
+                multiply_split(c, tp)
+                return
+            codes, scales = w_quantised[c]
+            if (c, tp) not in banks_open:
+                acc = mx_psum.tile([P, 2, ROWS], F32, tag="mx")
+                banks_open[(c, tp)] = acc
+            acc = banks_open[(c, tp)]
+            lo = 0 if h == WHOLE else h * P
+            hi = ROWS if h == WHOLE else (h + 1) * P
+            for tt in range(2):
+                for g in range(PASSES):
+                    xs = slice((2 * g + tt) * P, (2 * g + tt + 1) * P)
+                    ws = slice(g * ROWS + lo, g * ROWS + hi)
+                    nc.tensor.matmul_mx(
+                        out=acc[:, tt, lo:hi],
+                        lhsT=x_codes[:, tp, xs].bitcast(FP8X4),
+                        lhsT_scale=x_scales[:, tp, xs],
+                        rhs=codes[:, ws].bitcast(FP8X4),
+                        rhs_scale=scales[:, ws],
+                        start=(g == 0),
+                        stop=(g == PASSES - 1),
+                    )
+            if h == 0:
+                return
+            gi = group_of[c]
+            chunks = STORE_GROUPS[gi]
+            part = c - chunks[0]
+            wide = len(chunks) * ROWS
+            if (gi, tp) not in staged:
+                result = stage_pool.tile([P, 2, wide], F32, name="result_%d_%d" % (gi, tp))
+                staged[(gi, tp)] = result
+            result = staged[(gi, tp)]
+            bias_cols = bias_all[:, c * ROWS : (c + 1) * ROWS].unsqueeze(1).to_broadcast([P, 2, ROWS])
+            nc.vector.tensor_tensor(out=result[:, :, part * ROWS : (part + 1) * ROWS], in0=acc[:], in1=bias_cols, op=ADD)
+            if c == chunks[-1]:
+                first = chunks[0] * ROWS
+                nc.sync.dma_start(out=out_rows[:, 2 * tp : 2 * tp + 2, first : first + wide], in_=result[:])
+
+        have_x = []
+        have_w = []
+        pending = []
+        for i in range(len(units)):
+            prepare(i)
+            load_more()
+            if i == BIAS_AFTER:
+                spread_bias()
+            for c, h, tp in pending:
+                multiply(c, h, tp)
+            kind, n, h = units[i]
+            if kind == "x":
+                pending = [(c, hh, n) for c, hh in have_w]
+                have_x.append(n)
+            elif n in NARROW:
+                pending = [(n, h, tp) for tp in have_x]
+                have_w.append((n, h))
+            elif h != 0:
+                pending = [(n, WHOLE, tp) for tp in have_x]
+                have_w.append((n, WHOLE))
+            else:
+                pending = []
+        for c, h, tp in pending:
+            multiply(c, h, tp)

@@ -26,7 +26,7 @@ RAW_BUFS = 8
 HALF_BUFS = 8
 HALF_CHUNKS = 3
 NARROW = [1, 2]
-FINE_TO = 3
+FINE_TO = 2
 AHEAD_FROM = 1
 LAG = 1
 X_VECTOR_BANKS = []
@@ -60,6 +60,7 @@ def tile_sparselayer_kernel(tc, x, weights, bias, mask, out):
         const = ctx.enter_context(tc.tile_pool(name="const", bufs=1))
         raw_pool = ctx.enter_context(tc.tile_pool(name="raw", bufs=RAW_BUFS))
         half_pool = ctx.enter_context(tc.tile_pool(name="half", bufs=HALF_BUFS))
+        masked_pool = ctx.enter_context(tc.tile_pool(name="masked", bufs=2))
         grouped_pool = ctx.enter_context(tc.tile_pool(name="grouped", bufs=2))
         wq_pool = ctx.enter_context(tc.tile_pool(name="wq", bufs=3))
         stage_pool = ctx.enter_context(tc.tile_pool(name="stage", bufs=1))
@@ -133,6 +134,7 @@ def tile_sparselayer_kernel(tc, x, weights, bias, mask, out):
         x_scales = const.tile([P, N_PIECES, PASSES * ROWS], U8, align_bytes=64)
         w_quantised = {}
         grouped_of = {}
+        masked_of = {}
         staged = {}
         banks_open = {}
         mask_parts = {}
@@ -156,34 +158,42 @@ def tile_sparselayer_kernel(tc, x, weights, bias, mask, out):
                 return
             kind, n, h = units[i]
             w_raw, m_raw = raw[i]
+            if i not in masked_of:
+                masked = masked_pool.tile([P, n_banks(i) * 1024], BF16, tag="masked")
+                masked_of[i] = masked
+            masked = masked_of[i]
             for r in range(count):
                 if mask_parts[i] == 0:
                     return
                 b = n_banks(i) - mask_parts[i]
                 mask_parts[i] -= 1
-                if not is_fine(i):
-                    nc.vector.tensor_tensor(out=w_raw[:], in0=w_raw[:], in1=m_raw[:], op=MULT)
-                elif h == WHOLE:
-                    ks = slice(b * 512, (b + 1) * 512)
-                    w3 = w_raw[:].rearrange("p (s k) -> p s k", s=2)
-                    m3 = m_raw[:].rearrange("p (s k) -> p s k", s=2)
-                    nc.vector.tensor_tensor(out=w3[:, :, ks], in0=w3[:, :, ks], in1=m3[:, :, ks], op=MULT)
-                else:
-                    ks = slice(b * 1024, (b + 1) * 1024)
-                    nc.vector.tensor_tensor(out=w_raw[:, ks], in0=w_raw[:, ks], in1=m_raw[:, ks], op=MULT)
+                ks = slice(b * 1024, (b + 1) * 1024) if is_fine(i) else slice(0, 2 * K)
+                nc.vector.tensor_tensor(
+                    out=masked[:, ks].rearrange("p (u n e) -> p u n e", u=2, e=2),
+                    in0=w_raw[:, ks].rearrange("p (n u e) -> p u n e", u=2, e=2),
+                    in1=m_raw[:, ks].rearrange("p (n u e) -> p u n e", u=2, e=2),
+                    op=MULT,
+                )
                 if mask_parts[i] == 0:
-                    state[pool_of(i)] += 1
+                    state[pool_of(i)] += 2
 
         def fill_bank(i, b):
             kind, n, h = units[i]
-            words = raw[i][0][:].bitcast(F32)
             bank = tp_psum.tile([P, 4, P], F32, tag="tp")
             for q in range(4):
-                if h == WHOLE:
+                if kind == "x":
+                    words = raw[i][0][:].bitcast(F32)
                     first = (q // 2) * WORDS + b * 2 * P + q % 2
+                    picked = words[:, first : first + 2 * P - 1 : 2]
+                elif h == WHOLE:
+                    words = masked_of[i][:].bitcast(F32)
+                    first = (q % 2) * WORDS + (q // 2) * (WORDS // 2) + b * P
+                    picked = words[:, first : first + P]
                 else:
-                    first = (2 * b + q // 2) * 2 * P + q % 2
-                nc.tensor.transpose(out=bank[:, q, :], in_=words[:, first : first + 2 * P - 1 : 2], identity=ident[:])
+                    words = masked_of[i][:].bitcast(F32)
+                    first = b * 4 * P + (q % 2) * 2 * P + (q // 2) * P
+                    picked = words[:, first : first + P]
+                nc.tensor.transpose(out=bank[:, q, :], in_=picked, identity=ident[:])
             dst = grouped_of[i][:].bitcast(F32)[:, b * 512 : (b + 1) * 512]
             if kind == "w" and h == WHOLE:
                 nc.scalar.copy(out=dst.rearrange("p (j q) -> p j q", q=4), in_=bank[:].rearrange("p q j -> p j q"))
@@ -238,7 +248,8 @@ def tile_sparselayer_kernel(tc, x, weights, bias, mask, out):
                 for b in range(nb):
                     fill_bank(i, b)
                 quantise(i, None)
-            state[pool_of(i)] += 1
+            if kind == "x":
+                state[pool_of(i)] += 1
 
         def multiply_split(c, tp):
             codes, scales = w_quantised[c]

@@ -33,7 +33,7 @@ X_VECTOR_BANKS = []
 STORE_GROUPS = [[0, 1, 2, 3], [4, 5], [6], [7]]
 BIAS_AFTER = 0
 WARM_START = 6
-WARM = {1: 1, 2: 1}
+WARM = {}
 WHOLE = 2
 SPLIT_CELLS = [(7, 3)]
 

@@ -29,13 +29,14 @@ NARROW = [1, 2]
 FINE_TO = 2
 AHEAD_FROM = 1
 LAG = 1
+HOLD = [3, 5]
 X_VECTOR_BANKS = []
 STORE_GROUPS = [[0, 1, 2, 3], [4, 5], [6], [7]]
 BIAS_AFTER = 0
 WARM_START = 6
 WARM = {}
 WHOLE = 2
-SPLIT_CELLS = [(7, 3)]
+SPLIT_CELLS = [(7, 2), (7, 3)]
 
 
 def tile_sparselayer_kernel(tc, x, weights, bias, mask, out):
@@ -151,7 +152,7 @@ def tile_sparselayer_kernel(tc, x, weights, bias, mask, out):
 
         for i in range(len(units)):
             if units[i][0] == "w":
-                mask_parts[i] = n_banks(i) if is_fine(i) else 1
+                mask_parts[i] = 2
 
         def apply_mask(i, count):
             if i >= len(units) or units[i][0] == "x":
@@ -165,15 +166,23 @@ def tile_sparselayer_kernel(tc, x, weights, bias, mask, out):
             for r in range(count):
                 if mask_parts[i] == 0:
                     return
-                b = n_banks(i) - mask_parts[i]
+                b = 2 - mask_parts[i]
                 mask_parts[i] -= 1
-                ks = slice(b * 1024, (b + 1) * 1024) if is_fine(i) else slice(0, 2 * K)
-                nc.vector.tensor_tensor(
-                    out=masked[:, ks].rearrange("p (u n e) -> p u n e", u=2, e=2),
-                    in0=w_raw[:, ks].rearrange("p (n u e) -> p u n e", u=2, e=2),
-                    in1=m_raw[:, ks].rearrange("p (n u e) -> p u n e", u=2, e=2),
-                    op=MULT,
-                )
+                if is_fine(i):
+                    ks = slice(b * 1024, (b + 1) * 1024)
+                    nc.vector.tensor_tensor(
+                        out=masked[:, ks].rearrange("p (u n e) -> p u n e", u=2, e=2),
+                        in0=w_raw[:, ks].rearrange("p (n u e) -> p u n e", u=2, e=2),
+                        in1=m_raw[:, ks].rearrange("p (n u e) -> p u n e", u=2, e=2),
+                        op=MULT,
+                    )
+                else:
+                    nc.vector.tensor_tensor(
+                        out=masked[:, b * K : (b + 1) * K].rearrange("p (n e) -> p n e", e=2),
+                        in0=w_raw[:].rearrange("p (n u e) -> p u n e", u=2, e=2)[:, b],
+                        in1=m_raw[:].rearrange("p (n u e) -> p u n e", u=2, e=2)[:, b],
+                        op=MULT,
+                    )
                 if mask_parts[i] == 0:
                     state[pool_of(i)] += 2
 
@@ -244,9 +253,20 @@ def tile_sparselayer_kernel(tc, x, weights, bias, mask, out):
                 for b in range(nb - LAG, nb):
                     quantise(i, b)
             else:
-                apply_mask(i, 1)
+                apply_mask(i, 2)
+                words = masked_of[i][:].bitcast(F32)
+                banks = []
                 for b in range(nb):
-                    fill_bank(i, b)
+                    bank = tp_psum.tile([P, 4, P], F32, tag="tp")
+                    banks.append(bank)
+                for u in range(2):
+                    for b in range(nb):
+                        for row in range(2):
+                            first = u * WORDS + row * (WORDS // 2) + b * P
+                            nc.tensor.transpose(out=banks[b][:, 2 * row + u, :], in_=words[:, first : first + P], identity=ident[:])
+                        if u == 1:
+                            dst = grouped[:].bitcast(F32)[:, b * 512 : (b + 1) * 512]
+                            nc.scalar.copy(out=dst.rearrange("p (j q) -> p j q", q=4), in_=banks[b][:].rearrange("p q j -> p j q"))
                 quantise(i, None)
             if kind == "x":
                 state[pool_of(i)] += 1
@@ -319,19 +339,19 @@ def tile_sparselayer_kernel(tc, x, weights, bias, mask, out):
             load_more()
             if i == BIAS_AFTER:
                 spread_bias()
-            for c, h, tp in pending:
-                multiply(c, h, tp)
+            if i not in HOLD:
+                for c, h, tp in pending:
+                    multiply(c, h, tp)
+                pending = []
             kind, n, h = units[i]
             if kind == "x":
-                pending = [(c, hh, n) for c, hh in have_w]
+                pending.extend([(c, hh, n) for c, hh in have_w])
                 have_x.append(n)
             elif n in NARROW:
-                pending = [(n, h, tp) for tp in have_x]
+                pending.extend([(n, h, tp) for tp in have_x])
                 have_w.append((n, h))
             elif h != 0:
-                pending = [(n, WHOLE, tp) for tp in have_x]
+                pending.extend([(n, WHOLE, tp) for tp in have_x])
                 have_w.append((n, WHOLE))
-            else:
-                pending = []
         for c, h, tp in pending:
             multiply(c, h, tp)

@@ -75,6 +75,10 @@ def tile_sparselayer_kernel(tc, x, weights, bias, mask, out):
 
         raw = {}
         state = {"next_load": 0, "raw": RAW_BUFS, "half": HALF_BUFS}
+        ones = const.tile([P, P], BF16)
+        nc.vector.memset(ones[:], 1.0)
+        zeros = const.tile([P, 512], BF16)
+        nc.vector.memset(zeros[:], 0.0)
         bias_row = const.tile([P, FEAT], BF16)
         nc.vector.memset(bias_row[:], 0.0)
 
@@ -88,7 +92,7 @@ def tile_sparselayer_kernel(tc, x, weights, bias, mask, out):
                     return
                 state[pool_name] -= need
                 state["next_load"] += 1
-                if i == 1:
+                if i == 2:
                     nc.sync.dma_start(out=bias_row[0:1, :], in_=bias.rearrange("(o n) -> o n", o=1))
                 if kind == "x":
                     x_raw = raw_pool.tile([P, 2 * K], BF16, tag="raw")
@@ -110,10 +114,6 @@ def tile_sparselayer_kernel(tc, x, weights, bias, mask, out):
                     raw[i] = (w_raw, m_raw)
 
         load_more()
-        ones = const.tile([P, P], BF16)
-        nc.vector.memset(ones[:], 1.0)
-        zeros = const.tile([P, 512], BF16)
-        nc.vector.memset(zeros[:], 0.0)
         bias_all = const.tile([P, FEAT], BF16)
         junk = mx_psum.tile([P, 512], F32, tag="mx")
 

@@ -25,11 +25,11 @@ N_CHUNKS = FEAT // ROWS
 RAW_BUFS = 8
 HALF_BUFS = 8
 HALF_CHUNKS = 3
-NARROW = [1, 2]
+NARROW = [0, 1, 2]
 FINE_TO = 2
-AHEAD_FROM = 1
+AHEAD_FROM = 0
 LAG = 1
-HOLD = [3, 5]
+HOLD = []
 X_VECTOR_BANKS = []
 STORE_GROUPS = [[0, 1, 2, 3], [4, 5], [6], [7]]
 BIAS_AFTER = 0
@@ -49,7 +49,9 @@ def tile_sparselayer_kernel(tc, x, weights, bias, mask, out):
             return [("w", c, 0), ("w", c, 1)]
         return [("w", c, WHOLE)]
 
-    units = w_units(0) + [("x", tp, WHOLE) for tp in range(N_PIECES)]
+    first_w, second_w = w_units(0)
+    x_units = [("x", tp, WHOLE) for tp in range(N_PIECES)]
+    units = [x_units[0], first_w, x_units[1], second_w] + x_units[2:]
     for c in range(1, N_CHUNKS):
         units.extend(w_units(c))
     group_of = {}
@@ -92,7 +94,7 @@ def tile_sparselayer_kernel(tc, x, weights, bias, mask, out):
                     return
                 state[pool_name] -= need
                 state["next_load"] += 1
-                if i == 2:
+                if i == 1:
                     nc.sync.dma_start(out=bias_row[0:1, :], in_=bias.rearrange("(o n) -> o n", o=1))
                 if kind == "x":
                     x_raw = raw_pool.tile([P, 2 * K], BF16, tag="raw")
@@ -349,7 +351,9 @@ def tile_sparselayer_kernel(tc, x, weights, bias, mask, out):
                 have_x.append(n)
             elif n in NARROW:
                 pending.extend([(n, h, tp) for tp in have_x])
-                have_w.append((n, h))
+                if h == 1:
+                    have_w.remove((n, 0))
+                have_w.append((n, WHOLE if h == 1 else h))
             elif h != 0:
                 pending.extend([(n, WHOLE, tp) for tp in have_x])
                 have_w.append((n, WHOLE))

@@ -29,12 +29,13 @@ NARROW = [0, 1, 2]
 FINE_TO = 2
 AHEAD_FROM = 0
 LAG = 1
-HOLD = []
+QPOS = 1
+COPY_CHUNKS = [0, 1, 2, 3, 4, 5]
+QPOS_LAST = 2
 X_VECTOR_BANKS = []
 STORE_GROUPS = [[0, 1, 2, 3], [4, 5], [6], [7]]
 BIAS_AFTER = 0
 WARM_START = 6
-WARM = {}
 WHOLE = 2
 SPLIT_CELLS = [(7, 2), (7, 3)]
 
@@ -81,8 +82,12 @@ def tile_sparselayer_kernel(tc, x, weights, bias, mask, out):
         nc.vector.memset(ones[:], 1.0)
         zeros = const.tile([P, 512], BF16)
         nc.vector.memset(zeros[:], 0.0)
-        bias_row = const.tile([P, FEAT], BF16)
-        nc.vector.memset(bias_row[:], 0.0)
+        bias_rows = const.tile([P, 512], BF16)
+        nc.vector.memset(bias_rows[:], 0.0)
+        pick = const.tile([P, 4, P], BF16)
+        nc.vector.memset(pick[:], 0.0)
+        for r in range(4):
+            nc.vector.memset(pick[32 * r : 32 * r + 32, r, :], 1.0)
 
         def load_more():
             while state["next_load"] < len(units):
@@ -95,7 +100,7 @@ def tile_sparselayer_kernel(tc, x, weights, bias, mask, out):
                 state[pool_name] -= need
                 state["next_load"] += 1
                 if i == 1:
-                    nc.sync.dma_start(out=bias_row[0:1, :], in_=bias.rearrange("(o n) -> o n", o=1))
+                    nc.sync.dma_start(out=bias_rows[0:P:32, :], in_=bias.rearrange("(r n) -> r n", r=4))
                 if kind == "x":
                     x_raw = raw_pool.tile([P, 2 * K], BF16, tag="raw")
                     nc.sync.dma_start(out=x_raw[:], in_=x_rows[:, n * 2 * K : (n + 1) * 2 * K])
@@ -124,12 +129,10 @@ def tile_sparselayer_kernel(tc, x, weights, bias, mask, out):
                 nc.tensor.matmul(out=junk[:], lhsT=ones[:], rhs=zeros[:], start=True, stop=True)
 
         def spread_bias():
-            for b in range(FEAT // 1024):
-                spread = mx_psum.tile([P, 1024], BF16, tag="mx")
-                for hb in range(2):
-                    cols = slice(b * 1024 + hb * 512, b * 1024 + (hb + 1) * 512)
-                    nc.tensor.matmul(out=spread[:, hb * 512 : (hb + 1) * 512], lhsT=ones[:], rhs=bias_row[:, cols], start=True, stop=True)
-                nc.scalar.copy(out=bias_all[:, b * 1024 : (b + 1) * 1024], in_=spread[:])
+            for r in range(4):
+                spread = mx_psum.tile([P, 512], BF16, tag="mx")
+                nc.tensor.matmul(out=spread[:], lhsT=pick[:, r, :], rhs=bias_rows[:], start=True, stop=True)
+                nc.scalar.copy(out=bias_all[:, r * 512 : (r + 1) * 512], in_=spread[:])
 
         warm(WARM_START)
 
@@ -233,7 +236,7 @@ def tile_sparselayer_kernel(tc, x, weights, bias, mask, out):
                     cs = slice(g * ROWS + h * P, g * ROWS + (h + 1) * P)
                     nc.vector.quantize_mx(out=codes[:, cs].bitcast(FP8X4), scales=scales[:, cs], in_=grouped[:, g * 512 : (g + 1) * 512])
 
-        def prepare(i):
+        def prepare(i, cells):
             kind, n, h = units[i]
             nb = n_banks(i)
             grouped = grouped_pool.tile([P, nb * 1024], BF16, tag="grouped", align_bytes=64)
@@ -249,7 +252,6 @@ def tile_sparselayer_kernel(tc, x, weights, bias, mask, out):
                 for b in range(nb):
                     apply_mask(i, 1)
                     fill_bank(i, b)
-                    warm(WARM.get(i, 0))
                     if b >= LAG:
                         quantise(i, b - LAG)
                 for b in range(nb - LAG, nb):
@@ -269,6 +271,7 @@ def tile_sparselayer_kernel(tc, x, weights, bias, mask, out):
                         if u == 1:
                             dst = grouped[:].bitcast(F32)[:, b * 512 : (b + 1) * 512]
                             nc.scalar.copy(out=dst.rearrange("p (j q) -> p j q", q=4), in_=banks[b][:].rearrange("p q j -> p j q"))
+                multiply_next(cells, QPOS_LAST if i == len(units) - 1 else QPOS)
                 quantise(i, None)
             if kind == "x":
                 state[pool_of(i)] += 1
@@ -327,24 +330,45 @@ def tile_sparselayer_kernel(tc, x, weights, bias, mask, out):
                 result = stage_pool.tile([P, 2, wide], F32, name="result_%d_%d" % (gi, tp))
                 staged[(gi, tp)] = result
             result = staged[(gi, tp)]
+            if c in COPY_CHUNKS:
+                nc.scalar.copy(out=result[:, :, part * ROWS : (part + 1) * ROWS], in_=acc[:])
+                to_add.append((c, tp))
+            else:
+                add_bias(c, tp, acc[:])
+
+        def add_bias(c, tp, source):
+            gi = group_of[c]
+            chunks = STORE_GROUPS[gi]
+            part = c - chunks[0]
+            result = staged[(gi, tp)]
+            cell = result[:, :, part * ROWS : (part + 1) * ROWS]
             bias_cols = bias_all[:, c * ROWS : (c + 1) * ROWS].unsqueeze(1).to_broadcast([P, 2, ROWS])
-            nc.vector.tensor_tensor(out=result[:, :, part * ROWS : (part + 1) * ROWS], in0=acc[:], in1=bias_cols, op=ADD)
+            nc.vector.tensor_tensor(out=cell, in0=cell if source is None else source, in1=bias_cols, op=ADD)
             if c == chunks[-1]:
                 first = chunks[0] * ROWS
-                nc.sync.dma_start(out=out_rows[:, 2 * tp : 2 * tp + 2, first : first + wide], in_=result[:])
+                nc.sync.dma_start(out=out_rows[:, 2 * tp : 2 * tp + 2, first : first + len(chunks) * ROWS], in_=result[:])
 
+        def add_waiting():
+            while to_add:
+                c, tp = to_add.pop(0)
+                add_bias(c, tp, None)
+
+        def multiply_next(cells, count):
+            for r in range(min(count, len(cells))):
+                c, h, tp = cells.pop(0)
+                add_waiting()
+                multiply(c, h, tp)
+
+        to_add = []
         have_x = []
         have_w = []
         pending = []
         for i in range(len(units)):
-            prepare(i)
+            prepare(i, pending)
             load_more()
             if i == BIAS_AFTER:
                 spread_bias()
-            if i not in HOLD:
-                for c, h, tp in pending:
-                    multiply(c, h, tp)
-                pending = []
+            multiply_next(pending, len(pending))
             kind, n, h = units[i]
             if kind == "x":
                 pending.extend([(c, hh, n) for c, hh in have_w])
@@ -357,5 +381,5 @@ def tile_sparselayer_kernel(tc, x, weights, bias, mask, out):
             elif h != 0:
                 pending.extend([(n, WHOLE, tp) for tp in have_x])
                 have_w.append((n, WHOLE))
-        for c, h, tp in pending:
-            multiply(c, h, tp)
+        multiply_next(pending, len(pending))
+        add_waiting()

from contextlib import ExitStack

import concourse.mybir as mybir
from concourse.masks import make_identity

F32 = mybir.dt.float32
BF16 = mybir.dt.bfloat16
U32 = mybir.dt.uint32
U8 = mybir.dt.uint8
FP8X4 = mybir.dt.float8_e4m3fn_x4
ADD = mybir.AluOpType.add
MULT = mybir.AluOpType.mult

P = 128
BATCH = 1024
K = 2048
FEAT = 2048
FLOPS = 2 * BATCH * K * FEAT

PASSES = K // 512
ROWS = 256
WORDS = K // 2
N_PIECES = BATCH // ROWS
N_CHUNKS = FEAT // ROWS
RAW_BUFS = 8
HALF_BUFS = 8
HALF_CHUNKS = 3
NARROW = [0, 1, 2]
FINE_TO = 2
AHEAD_FROM = 0
LAG = 1
QPOS = 1
COPY_CHUNKS = [0, 1, 2, 3, 4, 5]
QPOS_LAST = 2
X_VECTOR_BANKS = []
STORE_GROUPS = [[0, 1, 2, 3], [4, 5], [6], [7]]
BIAS_AFTER = 0
WARM_START = 6
WHOLE = 2
SPLIT_CELLS = [(7, 2), (7, 3)]


def tile_sparselayer_kernel(tc, x, weights, bias, mask, out):
    nc = tc.nc
    x_rows = x.rearrange("(p t) k -> p (t k)", t=BATCH // P)
    out_rows = out.rearrange("(p t) n -> p t n", t=BATCH // P)

    def w_units(c):
        if c < HALF_CHUNKS:
            return [("w", c, 0), ("w", c, 1)]
        return [("w", c, WHOLE)]

    first_w, second_w = w_units(0)
    x_units = [("x", tp, WHOLE) for tp in range(N_PIECES)]
    units = [x_units[0], first_w, x_units[1], second_w] + x_units[2:]
    for c in range(1, N_CHUNKS):
        units.extend(w_units(c))
    group_of = {}
    for gi, chunks in enumerate(STORE_GROUPS):
        for c in chunks:
            group_of[c] = gi

    with ExitStack() as ctx:
        const = ctx.enter_context(tc.tile_pool(name="const", bufs=1))
        raw_pool = ctx.enter_context(tc.tile_pool(name="raw", bufs=RAW_BUFS))
        half_pool = ctx.enter_context(tc.tile_pool(name="half", bufs=HALF_BUFS))
        masked_pool = ctx.enter_context(tc.tile_pool(name="masked", bufs=2))
        grouped_pool = ctx.enter_context(tc.tile_pool(name="grouped", bufs=2))
        wq_pool = ctx.enter_context(tc.tile_pool(name="wq", bufs=3))
        stage_pool = ctx.enter_context(tc.tile_pool(name="stage", bufs=1))
        tp_psum = ctx.enter_context(tc.psum_pool(name="tp", bufs=4))
        mx_psum = ctx.enter_context(tc.psum_pool(name="mx", bufs=4))

        ident = const.tile([P, P], F32)
        make_identity(nc, ident[:])

        ctx.enter_context(tc.manual_schedule())

        raw = {}
        state = {"next_load": 0, "raw": RAW_BUFS, "half": HALF_BUFS}
        ones = const.tile([P, P], BF16)
        nc.vector.memset(ones[:], 1.0)
        zeros = const.tile([P, 512], BF16)
        nc.vector.memset(zeros[:], 0.0)
        bias_rows = const.tile([P, 512], BF16)
        nc.vector.memset(bias_rows[:], 0.0)
        pick = const.tile([P, 4, P], BF16)
        nc.vector.memset(pick[:], 0.0)
        for r in range(4):
            nc.vector.memset(pick[32 * r : 32 * r + 32, r, :], 1.0)

        def load_more():
            while state["next_load"] < len(units):
                i = state["next_load"]
                kind, n, h = units[i]
                pool_name = "raw" if h == WHOLE else "half"
                need = 1 if kind == "x" else 2
                if state[pool_name] < need:
                    return
                state[pool_name] -= need
                state["next_load"] += 1
                if i == 1:
                    nc.sync.dma_start(out=bias_rows[0:P:32, :], in_=bias.rearrange("(r n) -> r n", r=4))
                if kind == "x":
                    x_raw = raw_pool.tile([P, 2 * K], BF16, tag="raw")
                    nc.sync.dma_start(out=x_raw[:], in_=x_rows[:, n * 2 * K : (n + 1) * 2 * K])
                    raw[i] = (x_raw, None)
                elif h == WHOLE:
                    rows = slice(n * ROWS, (n + 1) * ROWS)
                    w_raw = raw_pool.tile([P, 2 * K], BF16, tag="raw")
                    nc.sync.dma_start(out=w_raw[:], in_=weights[rows, :].rearrange("(p s) k -> p (s k)", s=2))
                    m_raw = raw_pool.tile([P, 2 * K], BF16, tag="raw")
                    nc.sync.dma_start(out=m_raw[:], in_=mask[rows, :].rearrange("(p s) k -> p (s k)", s=2))
                    raw[i] = (w_raw, m_raw)
                else:
                    rows = slice(n * ROWS + h * P, n * ROWS + (h + 1) * P)
                    w_raw = half_pool.tile([P, K], BF16, tag="half")
                    nc.sync.dma_start(out=w_raw[:], in_=weights[rows, :])
                    m_raw = half_pool.tile([P, K], BF16, tag="half")
                    nc.sync.dma_start(out=m_raw[:], in_=mask[rows, :])
                    raw[i] = (w_raw, m_raw)

        load_more()
        bias_all = const.tile([P, FEAT], BF16)
        junk = mx_psum.tile([P, 512], F32, tag="mx")

        def warm(count):
            for r in range(count):
                nc.tensor.matmul(out=junk[:], lhsT=ones[:], rhs=zeros[:], start=True, stop=True)

        def spread_bias():
            for r in range(4):
                spread = mx_psum.tile([P, 512], BF16, tag="mx")
                nc.tensor.matmul(out=spread[:], lhsT=pick[:, r, :], rhs=bias_rows[:], start=True, stop=True)
                nc.scalar.copy(out=bias_all[:, r * 512 : (r + 1) * 512], in_=spread[:])

        warm(WARM_START)

        x_codes = const.tile([P, N_PIECES, PASSES * ROWS], U32, align_bytes=64)
        x_scales = const.tile([P, N_PIECES, PASSES * ROWS], U8, align_bytes=64)
        w_quantised = {}
        grouped_of = {}
        masked_of = {}
        staged = {}
        banks_open = {}
        mask_parts = {}

        def n_banks(i):
            return 4 if units[i][2] == WHOLE else 2

        def is_fine(i):
            kind, n, h = units[i]
            return kind == "x" or n <= FINE_TO

        def pool_of(i):
            return "raw" if units[i][2] == WHOLE else "half"

        for i in range(len(units)):
            if units[i][0] == "w":
                mask_parts[i] = 2

        def apply_mask(i, count):
            if i >= len(units) or units[i][0] == "x":
                return
            kind, n, h = units[i]
            w_raw, m_raw = raw[i]
            if i not in masked_of:
                masked = masked_pool.tile([P, n_banks(i) * 1024], BF16, tag="masked")
                masked_of[i] = masked
            masked = masked_of[i]
            for r in range(count):
                if mask_parts[i] == 0:
                    return
                b = 2 - mask_parts[i]
                mask_parts[i] -= 1
                if is_fine(i):
                    ks = slice(b * 1024, (b + 1) * 1024)
                    nc.vector.tensor_tensor(
                        out=masked[:, ks].rearrange("p (u n e) -> p u n e", u=2, e=2),
                        in0=w_raw[:, ks].rearrange("p (n u e) -> p u n e", u=2, e=2),
                        in1=m_raw[:, ks].rearrange("p (n u e) -> p u n e", u=2, e=2),
                        op=MULT,
                    )
                else:
                    nc.vector.tensor_tensor(
                        out=masked[:, b * K : (b + 1) * K].rearrange("p (n e) -> p n e", e=2),
                        in0=w_raw[:].rearrange("p (n u e) -> p u n e", u=2, e=2)[:, b],
                        in1=m_raw[:].rearrange("p (n u e) -> p u n e", u=2, e=2)[:, b],
                        op=MULT,
                    )
                if mask_parts[i] == 0:
                    state[pool_of(i)] += 2

        def fill_bank(i, b):
            kind, n, h = units[i]
            bank = tp_psum.tile([P, 4, P], F32, tag="tp")
            for q in range(4):
                if kind == "x":
                    words = raw[i][0][:].bitcast(F32)
                    first = (q // 2) * WORDS + b * 2 * P + q % 2
                    picked = words[:, first : first + 2 * P - 1 : 2]
                elif h == WHOLE:
                    words = masked_of[i][:].bitcast(F32)
                    first = (q % 2) * WORDS + (q // 2) * (WORDS // 2) + b * P
                    picked = words[:, first : first + P]
                else:
                    words = masked_of[i][:].bitcast(F32)
                    first = b * 4 * P + (q % 2) * 2 * P + (q // 2) * P
                    picked = words[:, first : first + P]
                nc.tensor.transpose(out=bank[:, q, :], in_=picked, identity=ident[:])
            dst = grouped_of[i][:].bitcast(F32)[:, b * 512 : (b + 1) * 512]
            if kind == "w" and h == WHOLE:
                nc.scalar.copy(out=dst.rearrange("p (j q) -> p j q", q=4), in_=bank[:].rearrange("p q j -> p j q"))
            else:
                dst = dst.rearrange("p (s j u) -> p s j u", s=2, u=2)
                src = bank[:].rearrange("p (s u) j -> p s j u", s=2)
                if kind == "x" and b in X_VECTOR_BANKS:
                    nc.vector.tensor_copy(out=dst, in_=src)
                else:
                    nc.scalar.copy(out=dst, in_=src)

        def quantise(i, b):
            kind, n, h = units[i]
            if kind == "x":
                codes, scales = x_codes[:, n, :], x_scales[:, n, :]
            else:
                codes, scales = w_quantised[n][0][:], w_quantised[n][1][:]
            grouped = grouped_of[i]
            if b is None:
                nc.vector.quantize_mx(out=codes.bitcast(FP8X4), scales=scales, in_=grouped[:])
            elif h == WHOLE:
                cs = slice(b * 256, (b + 1) * 256)
                nc.vector.quantize_mx(out=codes[:, cs].bitcast(FP8X4), scales=scales[:, cs], in_=grouped[:, b * 1024 : (b + 1) * 1024])
            else:
                for g in (2 * b, 2 * b + 1):
                    cs = slice(g * ROWS + h * P, g * ROWS + (h + 1) * P)
                    nc.vector.quantize_mx(out=codes[:, cs].bitcast(FP8X4), scales=scales[:, cs], in_=grouped[:, g * 512 : (g + 1) * 512])

        def prepare(i, cells):
            kind, n, h = units[i]
            nb = n_banks(i)
            grouped = grouped_pool.tile([P, nb * 1024], BF16, tag="grouped", align_bytes=64)
            grouped_of[i] = grouped
            if kind == "w" and n not in w_quantised:
                w_codes = wq_pool.tile([P, PASSES * ROWS], U32, tag="w_codes", align_bytes=64)
                w_scales = wq_pool.tile([P, PASSES * ROWS], U8, tag="w_scales", align_bytes=64)
                w_quantised[n] = (w_codes, w_scales)
            ahead = i + 1 < len(units) and units[i + 1][0] == "w" and units[i + 1][1] >= AHEAD_FROM
            if ahead:
                apply_mask(i + 1, 4)
            if is_fine(i):
                for b in range(nb):
                    apply_mask(i, 1)
                    fill_bank(i, b)
                    if b >= LAG:
                        quantise(i, b - LAG)
                for b in range(nb - LAG, nb):
                    quantise(i, b)
            else:
                apply_mask(i, 2)
                words = masked_of[i][:].bitcast(F32)
                banks = []
                for b in range(nb):
                    bank = tp_psum.tile([P, 4, P], F32, tag="tp")
                    banks.append(bank)
                for u in range(2):
                    for b in range(nb):
                        for row in range(2):
                            first = u * WORDS + row * (WORDS // 2) + b * P
                            nc.tensor.transpose(out=banks[b][:, 2 * row + u, :], in_=words[:, first : first + P], identity=ident[:])
                        if u == 1:
                            dst = grouped[:].bitcast(F32)[:, b * 512 : (b + 1) * 512]
                            nc.scalar.copy(out=dst.rearrange("p (j q) -> p j q", q=4), in_=banks[b][:].rearrange("p q j -> p j q"))
                multiply_next(cells, QPOS_LAST if i == len(units) - 1 else QPOS)
                quantise(i, None)
            if kind == "x":
                state[pool_of(i)] += 1

        def multiply_split(c, tp):
            codes, scales = w_quantised[c]
            for tt in range(2):
                small = mx_psum.tile([P, ROWS], F32, tag="mx")
                for g in range(PASSES):
                    xs = slice((2 * g + tt) * P, (2 * g + tt + 1) * P)
                    ws = slice(g * ROWS, (g + 1) * ROWS)
                    nc.tensor.matmul_mx(
                        out=small[:],
                        lhsT=x_codes[:, tp, xs].bitcast(FP8X4),
                        lhsT_scale=x_scales[:, tp, xs],
                        rhs=codes[:, ws].bitcast(FP8X4),
                        rhs_scale=scales[:, ws],
                        start=(g == 0),
                        stop=(g == PASSES - 1),
                    )
                last = stage_pool.tile([P, ROWS], F32, name="last_%d_%d_%d" % (c, tp, tt))
                nc.vector.tensor_tensor(out=last[:], in0=small[:], in1=bias_all[:, c * ROWS : (c + 1) * ROWS], op=ADD)
                nc.sync.dma_start(out=out_rows[:, 2 * tp + tt, c * ROWS : (c + 1) * ROWS], in_=last[:])

        def multiply(c, h, tp):
            if (c, tp) in SPLIT_CELLS:
                multiply_split(c, tp)
                return
            codes, scales = w_quantised[c]
            if (c, tp) not in banks_open:
                acc = mx_psum.tile([P, 2, ROWS], F32, tag="mx")
                banks_open[(c, tp)] = acc
            acc = banks_open[(c, tp)]
            lo = 0 if h == WHOLE else h * P
            hi = ROWS if h == WHOLE else (h + 1) * P
            for tt in range(2):
                for g in range(PASSES):
                    xs = slice((2 * g + tt) * P, (2 * g + tt + 1) * P)
                    ws = slice(g * ROWS + lo, g * ROWS + hi)
                    nc.tensor.matmul_mx(
                        out=acc[:, tt, lo:hi],
                        lhsT=x_codes[:, tp, xs].bitcast(FP8X4),
                        lhsT_scale=x_scales[:, tp, xs],
                        rhs=codes[:, ws].bitcast(FP8X4),
                        rhs_scale=scales[:, ws],
                        start=(g == 0),
                        stop=(g == PASSES - 1),
                    )
            if h == 0:
                return
            gi = group_of[c]
            chunks = STORE_GROUPS[gi]
            part = c - chunks[0]
            wide = len(chunks) * ROWS
            if (gi, tp) not in staged:
                result = stage_pool.tile([P, 2, wide], F32, name="result_%d_%d" % (gi, tp))
                staged[(gi, tp)] = result
            result = staged[(gi, tp)]
            if c in COPY_CHUNKS:
                nc.scalar.copy(out=result[:, :, part * ROWS : (part + 1) * ROWS], in_=acc[:])
                to_add.append((c, tp))
            else:
                add_bias(c, tp, acc[:])

        def add_bias(c, tp, source):
            gi = group_of[c]
            chunks = STORE_GROUPS[gi]
            part = c - chunks[0]
            result = staged[(gi, tp)]
            cell = result[:, :, part * ROWS : (part + 1) * ROWS]
            bias_cols = bias_all[:, c * ROWS : (c + 1) * ROWS].unsqueeze(1).to_broadcast([P, 2, ROWS])
            nc.vector.tensor_tensor(out=cell, in0=cell if source is None else source, in1=bias_cols, op=ADD)
            if c == chunks[-1]:
                first = chunks[0] * ROWS
                nc.sync.dma_start(out=out_rows[:, 2 * tp : 2 * tp + 2, first : first + len(chunks) * ROWS], in_=result[:])

        def add_waiting():
            while to_add:
                c, tp = to_add.pop(0)
                add_bias(c, tp, None)

        def multiply_next(cells, count):
            for r in range(min(count, len(cells))):
                c, h, tp = cells.pop(0)
                add_waiting()
                multiply(c, h, tp)

        to_add = []
        have_x = []
        have_w = []
        pending = []
        for i in range(len(units)):
            prepare(i, pending)
            load_more()
            if i == BIAS_AFTER:
                spread_bias()
            multiply_next(pending, len(pending))
            kind, n, h = units[i]
            if kind == "x":
                pending.extend([(c, hh, n) for c, hh in have_w])
                have_x.append(n)
            elif n in NARROW:
                pending.extend([(n, h, tp) for tp in have_x])
                if h == 1:
                    have_w.remove((n, 0))
                have_w.append((n, WHOLE if h == 1 else h))
            elif h != 0:
                pending.extend([(n, WHOLE, tp) for tp in have_x])
                have_w.append((n, WHOLE))
        multiply_next(pending, len(pending))
        add_waiting()
